import numpy as np
import ml_dtypes


def mxq(x, axis, fmt="e4m3"):
    dtype, down = {"e4m3": (ml_dtypes.float8_e4m3fn, 7), "e5m2": (ml_dtypes.float8_e5m2, 14)}[fmt]
    v = np.moveaxis(np.asarray(x, np.float32).astype(ml_dtypes.bfloat16).astype(np.float64), axis, -1)
    blocks = v.reshape(v.shape[:-1] + (-1, 32))
    amax = np.abs(blocks).max(-1, keepdims=True)
    byte = np.maximum(np.where(amax > 0, np.frexp(amax)[1] - 1 + 127, 0) - down, 1)
    scale = np.exp2(byte - 127.0)
    codes = (blocks / scale).astype(np.float32).astype(dtype).astype(np.float64)
    return np.moveaxis((codes * scale).reshape(v.shape), -1, axis)


WIDE = False


def mx_kscale(k):
    if not WIDE:
        return np.ones(k)
    levels = np.array([10, -10, 5, -5, 0])
    if k % 512:
        return np.exp2(np.random.permutation(np.resize(levels, k // 32))).repeat(32)
    a = np.empty((k // 512, 16))
    for p in range(k // 512):
        a[p, :8] = np.random.permutation(np.resize(levels, 8))
        for g in range(8):
            far = levels[np.abs(levels - a[p, g]) >= 10]
            a[p, g + 8] = far[np.random.randint(len(far))]
    return np.exp2(a.ravel()).repeat(32)


BF16 = ml_dtypes.bfloat16


def bf(x):
    return np.asarray(x, np.float32).astype(BF16)


def f64(x):
    return np.asarray(x).astype(np.float64)


B, T, C, N_HEAD, N_KV, HD, WINDOW = 1, 1024, 1024, 8, 2, 128, 512
QPK = N_HEAD // N_KV
TOT = QPK + 2
QKV_OUT = N_KV * TOT * HD


def apply_rope(xh, fc):
    b, t, h, d = xh.shape
    xs = xh.reshape(b, t, h, d // 2, 2)
    f = fc.reshape(1, t, 1, d // 2, 2)
    re = xs[..., 0] * f[..., 0] - xs[..., 1] * f[..., 1]
    im = xs[..., 1] * f[..., 0] + xs[..., 0] * f[..., 1]
    return np.stack([re, im], axis=-1).reshape(b, t, h, d)


def draw0():
    s = mx_kscale(C)
    inv_freq = 1.0 / (10000.0 ** (np.arange(0, HD, 2) / HD))
    ang = np.outer(np.arange(T), inv_freq)
    return {"x": bf(np.random.standard_normal((B, T, C)) * s),
            "freqs_cis": bf(np.stack([np.cos(ang), np.sin(ang)], axis=-1)),
            "W_attn": bf(np.random.standard_normal((C, QKV_OUT)) * 1.5 / np.sqrt(C) / s[:, None])}


def core(x, freqs_cis, W_attn):
    qkv = mxq(f64(x), 2, "e4m3") @ mxq(f64(W_attn), 0, "e4m3")
    qkv = qkv.reshape(B, T, N_KV, TOT, HD).transpose(0, 2, 3, 1, 4)
    q = qkv[:, :, :QPK].reshape(B, -1, N_HEAD, HD)
    k = qkv[:, :, QPK:QPK + 1].reshape(B, -1, N_KV, HD)
    v = qkv[:, :, QPK + 1:].reshape(B, -1, N_KV, HD)
    fc = f64(freqs_cis)
    return apply_rope(q, fc), apply_rope(k, fc), v


def e4m3fn_bytes(y):
    return np.clip(np.asarray(y, np.float64), -448.0, 448.0).astype(np.float32).astype(ml_dtypes.float8_e4m3fn).view(np.uint8)


def e4m3fn_values(b):
    return np.asarray(b, np.uint8).view(ml_dtypes.float8_e4m3fn).astype(np.float64)


def setup_inputs():
    d = draw0()
    x0 = np.asarray(d['W_attn']).astype(np.float64)
    s = (np.max(np.abs(x0), axis=(1,), keepdims=True) / 448.0).astype(np.float32)
    out = {}
    for k, v in d.items():
        if k == 'W_attn':
            out['W_attn_bytes'] = e4m3fn_bytes(x0 / s.astype(np.float64))
            out['W_attn_scale'] = s
        else:
            out[k] = v
    return out


def reference(x, freqs_cis, W_attn_bytes, W_attn_scale):
    return core(x, freqs_cis, e4m3fn_values(W_attn_bytes) * W_attn_scale.astype(np.float64))

@@ -1,0 +1,277 @@
+from contextlib import ExitStack
+
+import concourse.mybir as mybir
+from concourse.masks import make_identity
+
+F32 = mybir.dt.float32
+BF16 = mybir.dt.bfloat16
+U32 = mybir.dt.uint32
+U8 = mybir.dt.uint8
+FP8 = mybir.dt.float8_e4m3fn
+FP8X4 = mybir.dt.float8_e4m3fn_x4
+ALU = mybir.AluOpType
+ACT = mybir.ActivationFunctionType
+
+FLOPS = 2 * 1024 * 1024 * 1536
+
+P = 128
+NJ = 8
+JJ = 2
+
+
+def tile_causalselfattentiongqa_pa_kernel(tc, x, freqs_cis, W_attn_bytes, W_attn_scale, out_0, out_1, out_2):
+    nc = tc.nc
+    with ExitStack() as ctx:
+        const = ctx.enter_context(tc.tile_pool(name="const", bufs=1))
+        wpool = ctx.enter_context(tc.tile_pool(name="wpool", bufs=3))
+        xpool = ctx.enter_context(tc.tile_pool(name="xpool", bufs=3))
+        tpool = ctx.enter_context(tc.tile_pool(name="tpool", bufs=6))
+        opool = ctx.enter_context(tc.tile_pool(name="opool", bufs=3))
+        psum_t = ctx.enter_context(tc.psum_pool(name="psum_t", bufs=2))
+        psum_a = ctx.enter_context(tc.psum_pool(name="psum_a", bufs=6))
+
+        ident = const.tile([P, P], F32, name="ident")
+        make_identity(nc, ident[:])
+        sgn = const.tile([P, 512, 2], BF16, name="sgn")
+        nc.gpsimd.memset(sgn[:, :, 0:1], -1.0)
+        nc.gpsimd.memset(sgn[:, :, 1:2], 1.0)
+        warm = const.tile([P, 2], F32, name="warm")
+        nc.vector.memset(warm[:, 0:1], 0.0)
+        nc.scalar.activation(out=warm[:, 1:2], in_=warm[:, 0:1], func=ACT.Copy)
+
+        sc = const.tile([P, 2, 4], F32, name="sc")
+        nc.sync.dma_start(out=sc[:], in_=W_attn_scale.rearrange("(g p t) o -> p g (t o)", p=P, t=4))
+        wv = W_attn_bytes.rearrange("(g p t) n -> g p t n", p=P, t=4)
+        xv = x.rearrange("o (p j) k -> p (o j) k", j=NJ)
+        wby = {}
+        xin = {}
+
+        def load_w(b):
+            for g in range(2):
+                wt = const.tile([P, 4, 512], U8, name="wby%d_%d" % (b, g))
+                wby[(b, g)] = wt
+                if b == 0:
+                    nc.sync.dma_start(out=wt[:], in_=wv[g][:, :, 0:512])
+                elif b == 1:
+                    nc.sync.dma_start(out=wt[:], in_=wv[g][:, :, 768:1280])
+                else:
+                    nc.sync.dma_start(out=wt[:, :, 0:256], in_=wv[g][:, :, 512:768])
+                    nc.sync.dma_start(out=wt[:, :, 256:512], in_=wv[g][:, :, 1280:1536])
+
+        def load_x(j):
+            xt_in = const.tile([P, 1024], BF16, name="xin%d" % j)
+            xin[j] = xt_in
+            nc.sync.dma_start(out=xt_in[:], in_=xv[:, j, :])
+
+        fq = const.tile([P, 512, 2], BF16, name="fq")
+        fk = const.tile([P, 512, 2], BF16, name="fk")
+        load_w(0)
+        load_x(0)
+        load_x(1)
+        nc.sync.dma_start(out=fq[:].rearrange("p (s i) e -> p s (i e)", s=8),
+                          in_=freqs_cis.rearrange("(s p) i e -> p s (i e)", p=P))
+        load_w(1)
+        for j in range(2, NJ):
+            load_x(j)
+        nc.sync.dma_start(out=fk[:].rearrange("p (g c) e -> p g (c e)", g=2),
+                          in_=freqs_cis.rearrange("(g p a) i e -> p g (a i e)", p=P, a=4))
+        load_w(2)
+
+        wide = {}
+        wgr = {}
+        wc = {}
+        wsc = {}
+
+        def widen(eng, b, g, t):
+            if t == 0:
+                wide_t = wpool.tile([P, 4, 512], BF16, name="wide")
+                wide[(b, g)] = wide_t
+            src = wby[(b, g)][:, t, :].bitcast(FP8)
+            dst = wide[(b, g)][:, t, :]
+            s = sc[:, g, t:t + 1]
+            if eng == "v":
+                nc.vector.tensor_scalar(out=dst, in0=src, scalar1=s, scalar2=None, op0=ALU.mult)
+            else:
+                nc.scalar.activation(out=dst, in_=src, func=ACT.Copy, scale=s)
+
+        def interleave(eng, b, g):
+            wgr_t = wpool.tile([P, 512, 4], BF16, name="wgr", align_bytes=64)
+            wgr[(b, g)] = wgr_t
+            if b == 2:
+                for v in range(2):
+                    nc.scalar.copy(out=wgr_t[:, 256 * v:256 * (v + 1), :].rearrange("p (h f) t -> p h f t", h=2),
+                                   in_=wide[(b, g)][:].rearrange("p t (h v f) -> p t h v f", h=2, v=2)[:, :, :, v, :]
+                                   .rearrange("p t h f -> p h f t"))
+                return
+            src = wide[(b, g)][:].rearrange("p t (c i) -> p c t i", i=4)
+            dst = wgr_t[:].rearrange("p (c i) t -> p c t i", i=4)
+            if eng == "v":
+                nc.vector.tensor_copy(out=dst, in_=src)
+            else:
+                nc.scalar.copy(out=dst, in_=src)
+
+        def quant_w(b, g):
+            c = const.tile([P, 512], U32, name="wc%d_%d" % (b, g), align_bytes=64)
+            s = const.tile([P, 512], U8, name="ws%d_%d" % (b, g), align_bytes=64)
+            wc[(b, g)] = c
+            wsc[(b, g)] = s
+            nc.vector.quantize_mx(out=c[:].bitcast(FP8X4), scales=s[:],
+                                  in_=wgr[(b, g)][:].rearrange("p n t -> p (n t)"))
+
+        xg = {}
+        xc = {}
+        xsc = {}
+
+        def x_turn(j):
+            xt = psum_t.tile([P, 2, 2, P], F32, name="xt")
+            words = xin[j][:].bitcast(F32)
+            for g in range(2):
+                for u in range(2):
+                    nc.tensor.transpose(xt[:, g, u, :], words[:, 256 * g + u:256 * (g + 1):2], ident[:])
+            if j % 2 == 0:
+                xg_t = xpool.tile([P, 2048], BF16, name="xg", align_bytes=64)
+                xg[j // 2] = xg_t
+            half = xg[j // 2][:, 1024 * (j % 2):1024 * (j % 2 + 1)]
+            nc.scalar.copy(out=half.bitcast(F32).rearrange("p (g r u) -> p g r u", g=2, u=2),
+                           in_=xt[:].rearrange("p g u r -> p g r u"))
+
+        def x_quant(a):
+            c = const.tile([P, 512], U32, name="xc%d" % a, align_bytes=64)
+            s = const.tile([P, 512], U8, name="xs%d" % a, align_bytes=64)
+            xc[a] = c
+            xsc[a] = s
+            nc.vector.quantize_mx(out=c[:].bitcast(FP8X4), scales=s[:], in_=xg[a][:])
+
+        def x_cols(j, g):
+            return slice(256 * (j % 2) + P * g, 256 * (j % 2) + P * (g + 1))
+
+        sq = const.tile([P, 512, 2], BF16, name="sq")
+        sk = const.tile([P, 512, 2], BF16, name="sk")
+        qv = out_0.rearrange("o (s p) h f -> p (o s) (h f)", p=P)
+        kv = out_1.rearrange("o (g p a) h f -> p (o g) (a h f)", p=P, a=4)
+        vv = out_2.rearrange("o (g p a) h f -> p (o g) (a h f)", p=P, a=4)
+
+        def mm(b, j):
+            acc = psum_a.tile([P, 512], F32, name="acc")
+            for g in range(2):
+                nc.tensor.matmul_mx(out=acc[:],
+                                    lhsT=xc[j // 2][:, x_cols(j, g)].bitcast(FP8X4),
+                                    lhsT_scale=xsc[j // 2][:, x_cols(j, g)],
+                                    rhs=wc[(b, g)][:].bitcast(FP8X4),
+                                    rhs_scale=wsc[(b, g)][:],
+                                    start=(g == 0), stop=(g == 1))
+            return acc
+
+        stage = {}
+
+        def rope_q(b, j, acc):
+            jj = j % JJ
+            if jj == 0:
+                oq_t = opool.tile([P, 4, JJ * P], F32, name="oq")
+                stage["q"] = oq_t
+            oq = stage["q"]
+            t1 = tpool.tile([P, 256, 2], F32, name="t1")
+            t2 = tpool.tile([P, 256, 2], F32, name="t2")
+            av = acc[:].rearrange("p (c e) -> p c e", e=2)
+            nc.vector.tensor_tensor(out=t1[:], in0=fq[:, 256 * b:256 * (b + 1), 0:1].to_broadcast([P, 256, 2]),
+                                    in1=av, op=ALU.mult)
+            nc.vector.tensor_tensor(out=t2[:], in0=sq[:, 256 * b:256 * (b + 1), :],
+                                    in1=av[:, :, ::-1], op=ALU.mult)
+            nc.gpsimd.tensor_tensor(out=oq[:, :, jj * P:(jj + 1) * P],
+                                    in0=t1[:].rearrange("p (s i) e -> p s (i e)", s=4),
+                                    in1=t2[:].rearrange("p (s i) e -> p s (i e)", s=4), op=ALU.add)
+            if jj == JJ - 1:
+                j0 = j - jj
+                nc.sync.dma_start(out=qv[:, 4 * b:4 * (b + 1), j0 * P:(j + 1) * P], in_=oq[:])
+
+        ck = const.tile([P, 512, 2], BF16, name="ck")
+
+        def kv_pair(a, adder):
+            acc_k = psum_a.tile([P, 2, 256], F32, name="acc")
+            acc_v = psum_a.tile([P, 2, 256], F32, name="acc")
+            for jj in range(2):
+                j = 2 * a + jj
+                for v, acc in ((0, acc_k), (1, acc_v)):
+                    for g in range(2):
+                        nc.tensor.matmul_mx(out=acc[:, jj, :],
+                                            lhsT=xc[a][:, x_cols(j, g)].bitcast(FP8X4),
+                                            lhsT_scale=xsc[a][:, x_cols(j, g)],
+                                            rhs=wc[(2, g)][:, 256 * v:256 * (v + 1)].bitcast(FP8X4),
+                                            rhs_scale=wsc[(2, g)][:, 256 * v:256 * (v + 1)],
+                                            start=(g == 0), stop=(g == 1))
+            ok = opool.tile([P, 2, 2, P], F32, name="ok")
+            ov = opool.tile([P, 2, 2, P], F32, name="ov")
+            t1 = tpool.tile([P, 512], F32, name="t1")
+            t2 = tpool.tile([P, 512], F32, name="t2")
+            ckv = ck[:].rearrange("p (h a i) e -> p h a (i e)", h=2, a=4)[:, :, a, :].unsqueeze(1).to_broadcast([P, 2, 2, P])
+            skv = sk[:].rearrange("p (h a i) e -> p h a (i e)", h=2, a=4)[:, :, a, :].unsqueeze(1).to_broadcast([P, 2, 2, P])
+            nc.vector.tensor_tensor(out=t1[:].rearrange("p (j h f) -> p j h f", j=2, h=2),
+                                    in0=ckv, in1=acc_k[:].rearrange("p j (h f) -> p j h f", h=2), op=ALU.mult)
+            nc.vector.tensor_tensor(out=t2[:].rearrange("p (j h f) -> p j h f", j=2, h=2),
+                                    in0=skv, in1=acc_k[:].rearrange("p j (c e) -> p (j c) e", e=2)[:, :, ::-1], op=ALU.mult)
+            nc.scalar.copy(out=ov[:], in_=acc_v[:].rearrange("p j (h f) -> p h j f", h=2))
+            okv = ok[:].rearrange("p h j f -> p j h f")
+            t1v = t1[:].rearrange("p (j h f) -> p j h f", j=2, h=2)
+            t2v = t2[:].rearrange("p (j h f) -> p j h f", j=2, h=2)
+            if adder == "g":
+                nc.gpsimd.tensor_tensor(out=okv, in0=t1v, in1=t2v, op=ALU.add)
+            elif adder == "v":
+                nc.vector.tensor_tensor(out=okv, in0=t1v, in1=t2v, op=ALU.add)
+            else:
+                acc2 = psum_t.tile([P, 512], F32, name="xt")
+                nc.tensor.matmul(out=acc2[:], lhsT=ident[:], rhs=t1[:], start=True, stop=False)
+                nc.tensor.matmul(out=acc2[:], lhsT=ident[:], rhs=t2[:], start=False, stop=True)
+                nc.scalar.copy(out=okv, in_=acc2[:].rearrange("p (j h f) -> p j h f", j=2, h=2))
+            cols = slice(2 * a * P, 2 * (a + 1) * P)
+            nc.sync.dma_start(out=vv[:, :, cols], in_=ov[:].rearrange("p h j f -> p h (j f)"))
+            nc.sync.dma_start(out=kv[:, :, cols], in_=ok[:].rearrange("p h j f -> p h (j f)"))
+
+        for t in range(4):
+            widen("v", 0, 0, t)
+        widen("v", 0, 1, 0)
+        for t in range(1, 4):
+            widen("s", 0, 1, t)
+        x_turn(0)
+        x_turn(1)
+        interleave("v", 0, 0)
+        interleave("v", 0, 1)
+        x_quant(0)
+        quant_w(0, 0)
+        quant_w(0, 1)
+        nc.gpsimd.tensor_tensor(out=sq[:], in0=fq[:, :, 1:2].to_broadcast([P, 512, 2]), in1=sgn[:], op=ALU.mult)
+        nc.gpsimd.tensor_tensor(out=sk[:], in0=fk[:, :, 1:2].to_broadcast([P, 512, 2]), in1=sgn[:], op=ALU.mult)
+        nc.gpsimd.tensor_scalar(out=ck[:], in0=fk[:, :, 0:1].to_broadcast([P, 512, 2]), scalar1=1.0, scalar2=0.0,
+                                op0=ALU.mult, op1=ALU.add)
+
+        def prep_items(b):
+            items = []
+            for g in range(2):
+                for t in range(4):
+                    items.append(("w", b, g, t))
+                items.append(("i", b, g, 0))
+                items.append(("q", b, g, 0))
+            return items
+
+        def run_item(it):
+            kind, b, g, t = it
+            if kind == "w":
+                widen("s", b, g, t)
+            elif kind == "i":
+                interleave("v" if (b == 1 and g == 0) else "s", b, g)
+            else:
+                quant_w(b, g)
+
+        for b in range(2):
+            items = prep_items(b + 1)
+            for j in range(NJ):
+                if b == 0 and j % 2 == 0 and j + 2 < NJ:
+                    x_turn(j + 2)
+                    x_turn(j + 3)
+                    x_quant(j // 2 + 1)
+                acc = mm(b, j)
+                rope_q(b, j, acc)
+                for n in range(2):
+                    if items:
+                        run_item(items.pop(0))
+        for a, adder in enumerate(("g", "g", "g", "v")):
+            kv_pair(a, adder)

@@ -239,9 +239,6 @@ def tile_causalselfattentiongqa_pa_kernel(tc, x, freqs_cis, W_attn_bytes, W_attn
         quant_w(0, 0)
         quant_w(0, 1)
         nc.gpsimd.tensor_tensor(out=sq[:], in0=fq[:, :, 1:2].to_broadcast([P, 512, 2]), in1=sgn[:], op=ALU.mult)
-        nc.gpsimd.tensor_tensor(out=sk[:], in0=fk[:, :, 1:2].to_broadcast([P, 512, 2]), in1=sgn[:], op=ALU.mult)
-        nc.gpsimd.tensor_scalar(out=ck[:], in0=fk[:, :, 0:1].to_broadcast([P, 512, 2]), scalar1=1.0, scalar2=0.0,
-                                op0=ALU.mult, op1=ALU.add)
 
         def prep_items(b):
             items = []
@@ -263,6 +260,10 @@ def tile_causalselfattentiongqa_pa_kernel(tc, x, freqs_cis, W_attn_bytes, W_attn
 
         for b in range(2):
             items = prep_items(b + 1)
+            if b == 1:
+                nc.scalar.activation(out=sk[:, :, 0:1], in_=fk[:, :, 1:2], func=ACT.Copy, scale=-1.0)
+                nc.scalar.copy(out=sk[:, :, 1:2], in_=fk[:, :, 1:2])
+                nc.scalar.copy(out=ck[:], in_=fk[:, :, 0:1].to_broadcast([P, 512, 2]))
             for j in range(NJ):
                 if b == 0 and j % 2 == 0 and j + 2 < NJ:
                     x_turn(j + 2)

@@ -32,9 +32,8 @@ def tile_causalselfattentiongqa_pa_kernel(tc, x, freqs_cis, W_attn_bytes, W_attn
 
         ident = const.tile([P, P], F32, name="ident")
         make_identity(nc, ident[:])
-        sgn = const.tile([P, 512, 2], BF16, name="sgn")
-        nc.gpsimd.memset(sgn[:, :, 0:1], -1.0)
-        nc.gpsimd.memset(sgn[:, :, 1:2], 1.0)
+        heat = const.tile([P, 512], BF16, name="heat")
+        nc.vector.memset(heat[:], 0.0)
         warm = const.tile([P, 2], F32, name="warm")
         nc.vector.memset(warm[:, 0:1], 0.0)
         nc.scalar.activation(out=warm[:, 1:2], in_=warm[:, 0:1], func=ACT.Copy)
@@ -63,12 +62,13 @@ def tile_causalselfattentiongqa_pa_kernel(tc, x, freqs_cis, W_attn_bytes, W_attn
             xin[j] = xt_in
             nc.sync.dma_start(out=xt_in[:], in_=xv[:, j, :])
 
-        fq = const.tile([P, 512, 2], BF16, name="fq")
+        fq2 = const.tile([P, 2, 512, 2], BF16, name="fq2")
+        fq = fq2[:, 0, :, :]
         fk = const.tile([P, 512, 2], BF16, name="fk")
         load_w(0)
         load_x(0)
         load_x(1)
-        nc.sync.dma_start(out=fq[:].rearrange("p (s i) e -> p s (i e)", s=8),
+        nc.sync.dma_start(out=fq.rearrange("p (s i) e -> p s (i e)", s=8),
                           in_=freqs_cis.rearrange("(s p) i e -> p s (i e)", p=P))
         load_w(1)
         for j in range(2, NJ):
@@ -135,17 +135,19 @@ def tile_causalselfattentiongqa_pa_kernel(tc, x, freqs_cis, W_attn_bytes, W_attn
             nc.scalar.copy(out=half.bitcast(F32).rearrange("p (g r u) -> p g r u", g=2, u=2),
                            in_=xt[:].rearrange("p g u r -> p g r u"))
 
-        def x_quant(a):
+        def x_quant(a, parts=1):
             c = const.tile([P, 512], U32, name="xc%d" % a, align_bytes=64)
             s = const.tile([P, 512], U8, name="xs%d" % a, align_bytes=64)
             xc[a] = c
             xsc[a] = s
-            nc.vector.quantize_mx(out=c[:].bitcast(FP8X4), scales=s[:], in_=xg[a][:])
+            w = 512 // parts
+            for h in range(parts):
+                nc.vector.quantize_mx(out=c[:, w * h:w * (h + 1)].bitcast(FP8X4), scales=s[:, w * h:w * (h + 1)],
+                                      in_=xg[a][:, 4 * w * h:4 * w * (h + 1)])
 
         def x_cols(j, g):
             return slice(256 * (j % 2) + P * g, 256 * (j % 2) + P * (g + 1))
 
-        sq = const.tile([P, 512, 2], BF16, name="sq")
         sk = const.tile([P, 512, 2], BF16, name="sk")
         qv = out_0.rearrange("o (s p) h f -> p (o s) (h f)", p=P)
         kv = out_1.rearrange("o (g p a) h f -> p (o g) (a h f)", p=P, a=4)
@@ -175,7 +177,7 @@ def tile_causalselfattentiongqa_pa_kernel(tc, x, freqs_cis, W_attn_bytes, W_attn
             av = acc[:].rearrange("p (c e) -> p c e", e=2)
             nc.vector.tensor_tensor(out=t1[:], in0=fq[:, 256 * b:256 * (b + 1), 0:1].to_broadcast([P, 256, 2]),
                                     in1=av, op=ALU.mult)
-            nc.vector.tensor_tensor(out=t2[:], in0=sq[:, 256 * b:256 * (b + 1), :],
+            nc.vector.tensor_tensor(out=t2[:], in0=fq2[:, ::-1, 256 * b:256 * (b + 1), 1].rearrange("p h c -> p c h"),
                                     in1=av[:, :, ::-1], op=ALU.mult)
             nc.gpsimd.tensor_tensor(out=oq[:, :, jj * P:(jj + 1) * P],
                                     in0=t1[:].rearrange("p (s i) e -> p s (i e)", s=4),
@@ -226,6 +228,9 @@ def tile_causalselfattentiongqa_pa_kernel(tc, x, freqs_cis, W_attn_bytes, W_attn
             nc.sync.dma_start(out=vv[:, :, cols], in_=ov[:].rearrange("p h j f -> p h (j f)"))
             nc.sync.dma_start(out=kv[:, :, cols], in_=ok[:].rearrange("p h j f -> p h (j f)"))
 
+        hot = psum_t.tile([P, 512], F32, name="xt")
+        for n in range(6):
+            nc.tensor.matmul(out=hot[:], lhsT=heat[:, 0:P], rhs=heat[:], start=True, stop=True)
         for t in range(4):
             widen("v", 0, 0, t)
         widen("v", 0, 1, 0)
@@ -235,10 +240,10 @@ def tile_causalselfattentiongqa_pa_kernel(tc, x, freqs_cis, W_attn_bytes, W_attn
         x_turn(1)
         interleave("v", 0, 0)
         interleave("v", 0, 1)
-        x_quant(0)
+        x_quant(0, parts=2)
         quant_w(0, 0)
         quant_w(0, 1)
-        nc.gpsimd.tensor_tensor(out=sq[:], in0=fq[:, :, 1:2].to_broadcast([P, 512, 2]), in1=sgn[:], op=ALU.mult)
+        nc.scalar.activation(out=fq2[:, 1, :, 1:2], in_=fq2[:, 0, :, 1:2], func=ACT.Copy, scale=-1.0)
 
         def prep_items(b):
             items = []

@@ -25,8 +25,8 @@ def tile_causalselfattentiongqa_pa_kernel(tc, x, freqs_cis, W_attn_bytes, W_attn
         const = ctx.enter_context(tc.tile_pool(name="const", bufs=1))
         wpool = ctx.enter_context(tc.tile_pool(name="wpool", bufs=3))
         xpool = ctx.enter_context(tc.tile_pool(name="xpool", bufs=3))
-        tpool = ctx.enter_context(tc.tile_pool(name="tpool", bufs=6))
-        opool = ctx.enter_context(tc.tile_pool(name="opool", bufs=3))
+        tpool = ctx.enter_context(tc.tile_pool(name="tpool", bufs=12))
+        opool = ctx.enter_context(tc.tile_pool(name="opool", bufs=5))
         psum_t = ctx.enter_context(tc.psum_pool(name="psum_t", bufs=2))
         psum_a = ctx.enter_context(tc.psum_pool(name="psum_a", bufs=6))
 
@@ -188,7 +188,7 @@ def tile_causalselfattentiongqa_pa_kernel(tc, x, freqs_cis, W_attn_bytes, W_attn
 
         ck = const.tile([P, 512, 2], BF16, name="ck")
 
-        def kv_pair(a, adder):
+        def kv_pair(a):
             acc_k = psum_a.tile([P, 2, 256], F32, name="acc")
             acc_v = psum_a.tile([P, 2, 256], F32, name="acc")
             for jj in range(2):
@@ -215,18 +215,13 @@ def tile_causalselfattentiongqa_pa_kernel(tc, x, freqs_cis, W_attn_bytes, W_attn
             okv = ok[:].rearrange("p h j f -> p j h f")
             t1v = t1[:].rearrange("p (j h f) -> p j h f", j=2, h=2)
             t2v = t2[:].rearrange("p (j h f) -> p j h f", j=2, h=2)
-            if adder == "g":
-                nc.gpsimd.tensor_tensor(out=okv, in0=t1v, in1=t2v, op=ALU.add)
-            elif adder == "v":
-                nc.vector.tensor_tensor(out=okv, in0=t1v, in1=t2v, op=ALU.add)
-            else:
-                acc2 = psum_t.tile([P, 512], F32, name="xt")
-                nc.tensor.matmul(out=acc2[:], lhsT=ident[:], rhs=t1[:], start=True, stop=False)
-                nc.tensor.matmul(out=acc2[:], lhsT=ident[:], rhs=t2[:], start=False, stop=True)
-                nc.scalar.copy(out=okv, in_=acc2[:].rearrange("p (j h f) -> p j h f", j=2, h=2))
             cols = slice(2 * a * P, 2 * (a + 1) * P)
             nc.sync.dma_start(out=vv[:, :, cols], in_=ov[:].rearrange("p h j f -> p h (j f)"))
-            nc.sync.dma_start(out=kv[:, :, cols], in_=ok[:].rearrange("p h j f -> p h (j f)"))
+
+            def finish():
+                nc.vector.tensor_tensor(out=okv, in0=t1v, in1=t2v, op=ALU.add)
+                nc.sync.dma_start(out=kv[:, :, cols], in_=ok[:].rearrange("p h j f -> p h (j f)"))
+            return finish
 
         hot = psum_t.tile([P, 512], F32, name="xt")
         for n in range(6):
@@ -279,5 +274,9 @@ def tile_causalselfattentiongqa_pa_kernel(tc, x, freqs_cis, W_attn_bytes, W_attn
                 for n in range(2):
                     if items:
                         run_item(items.pop(0))
-        for a, adder in enumerate(("g", "g", "g", "v")):
-            kv_pair(a, adder)
+        pending = []
+        for a in range(4):
+            pending.append(kv_pair(a))
+            if a > 0:
+                pending.pop(0)()
+        pending.pop(0)()

@@ -27,8 +27,7 @@ def tile_causalselfattentiongqa_pa_kernel(tc, x, freqs_cis, W_attn_bytes, W_attn
         xpool = ctx.enter_context(tc.tile_pool(name="xpool", bufs=3))
         tpool = ctx.enter_context(tc.tile_pool(name="tpool", bufs=12))
         opool = ctx.enter_context(tc.tile_pool(name="opool", bufs=5))
-        psum_t = ctx.enter_context(tc.psum_pool(name="psum_t", bufs=2))
-        psum_a = ctx.enter_context(tc.psum_pool(name="psum_a", bufs=6))
+        psum = ctx.enter_context(tc.psum_pool(name="psum", bufs=8))
 
         ident = const.tile([P, P], F32, name="ident")
         make_identity(nc, ident[:])
@@ -123,7 +122,7 @@ def tile_causalselfattentiongqa_pa_kernel(tc, x, freqs_cis, W_attn_bytes, W_attn
         xsc = {}
 
         def x_turn(j):
-            xt = psum_t.tile([P, 2, 2, P], F32, name="xt")
+            xt = psum.tile([P, 2, 2, P], F32, name="acc")
             words = xin[j][:].bitcast(F32)
             for g in range(2):
                 for u in range(2):
@@ -135,15 +134,13 @@ def tile_causalselfattentiongqa_pa_kernel(tc, x, freqs_cis, W_attn_bytes, W_attn
             nc.scalar.copy(out=half.bitcast(F32).rearrange("p (g r u) -> p g r u", g=2, u=2),
                            in_=xt[:].rearrange("p g u r -> p g r u"))
 
-        def x_quant(a, parts=1):
-            c = const.tile([P, 512], U32, name="xc%d" % a, align_bytes=64)
-            s = const.tile([P, 512], U8, name="xs%d" % a, align_bytes=64)
-            xc[a] = c
-            xsc[a] = s
-            w = 512 // parts
-            for h in range(parts):
-                nc.vector.quantize_mx(out=c[:, w * h:w * (h + 1)].bitcast(FP8X4), scales=s[:, w * h:w * (h + 1)],
-                                      in_=xg[a][:, 4 * w * h:4 * w * (h + 1)])
+        def x_quant(a, lo=0, hi=512):
+            if a not in xc:
+                c_t = const.tile([P, 512], U32, name="xc%d" % a, align_bytes=64)
+                s_t = const.tile([P, 512], U8, name="xs%d" % a, align_bytes=64)
+                xc[a] = c_t
+                xsc[a] = s_t
+            nc.vector.quantize_mx(out=xc[a][:, lo:hi].bitcast(FP8X4), scales=xsc[a][:, lo:hi], in_=xg[a][:, 4 * lo:4 * hi])
 
         def x_cols(j, g):
             return slice(256 * (j % 2) + P * g, 256 * (j % 2) + P * (g + 1))
@@ -154,7 +151,7 @@ def tile_causalselfattentiongqa_pa_kernel(tc, x, freqs_cis, W_attn_bytes, W_attn
         vv = out_2.rearrange("o (g p a) h f -> p (o g) (a h f)", p=P, a=4)
 
         def mm(b, j):
-            acc = psum_a.tile([P, 512], F32, name="acc")
+            acc = psum.tile([P, 512], F32, name="acc")
             for g in range(2):
                 nc.tensor.matmul_mx(out=acc[:],
                                     lhsT=xc[j // 2][:, x_cols(j, g)].bitcast(FP8X4),
@@ -189,8 +186,8 @@ def tile_causalselfattentiongqa_pa_kernel(tc, x, freqs_cis, W_attn_bytes, W_attn
         ck = const.tile([P, 512, 2], BF16, name="ck")
 
         def kv_pair(a):
-            acc_k = psum_a.tile([P, 2, 256], F32, name="acc")
-            acc_v = psum_a.tile([P, 2, 256], F32, name="acc")
+            acc_k = psum.tile([P, 2, 256], F32, name="acc")
+            acc_v = psum.tile([P, 2, 256], F32, name="acc")
             for jj in range(2):
                 j = 2 * a + jj
                 for v, acc in ((0, acc_k), (1, acc_v)):
@@ -223,7 +220,7 @@ def tile_causalselfattentiongqa_pa_kernel(tc, x, freqs_cis, W_attn_bytes, W_attn
                 nc.sync.dma_start(out=kv[:, :, cols], in_=ok[:].rearrange("p h j f -> p h (j f)"))
             return finish
 
-        hot = psum_t.tile([P, 512], F32, name="xt")
+        hot = psum.tile([P, 512], F32, name="acc")
         for n in range(6):
             nc.tensor.matmul(out=hot[:], lhsT=heat[:, 0:P], rhs=heat[:], start=True, stop=True)
         for t in range(4):
@@ -233,10 +230,19 @@ def tile_causalselfattentiongqa_pa_kernel(tc, x, freqs_cis, W_attn_bytes, W_attn
             widen("s", 0, 1, t)
         x_turn(0)
         x_turn(1)
+
+        def keep_hot(g):
+            for n in range(3):
+                nc.tensor.matmul(out=hot[:], lhsT=heat[:, 0:P], rhs=wgr[(0, g)][:, 0:P, :].rearrange("p n t -> p (n t)"),
+                                 start=True, stop=True)
+
         interleave("v", 0, 0)
-        interleave("v", 0, 1)
-        x_quant(0, parts=2)
+        keep_hot(0)
+        x_quant(0, 0, 256)
         quant_w(0, 0)
+        interleave("v", 0, 1)
+        keep_hot(1)
+        x_quant(0, 256, 512)
         quant_w(0, 1)
         nc.scalar.activation(out=fq2[:, 1, :, 1:2], in_=fq2[:, 0, :, 1:2], func=ACT.Copy, scale=-1.0)
 

from contextlib import ExitStack

import concourse.mybir as mybir
from concourse.masks import make_identity

F32 = mybir.dt.float32
BF16 = mybir.dt.bfloat16
U32 = mybir.dt.uint32
U8 = mybir.dt.uint8
FP8 = mybir.dt.float8_e4m3fn
FP8X4 = mybir.dt.float8_e4m3fn_x4
ALU = mybir.AluOpType
ACT = mybir.ActivationFunctionType

FLOPS = 2 * 1024 * 1024 * 1536

P = 128
NJ = 8
JJ = 2


def tile_causalselfattentiongqa_pa_kernel(tc, x, freqs_cis, W_attn_bytes, W_attn_scale, out_0, out_1, out_2):
    nc = tc.nc
    with ExitStack() as ctx:
        const = ctx.enter_context(tc.tile_pool(name="const", bufs=1))
        wpool = ctx.enter_context(tc.tile_pool(name="wpool", bufs=3))
        xpool = ctx.enter_context(tc.tile_pool(name="xpool", bufs=3))
        tpool = ctx.enter_context(tc.tile_pool(name="tpool", bufs=12))
        opool = ctx.enter_context(tc.tile_pool(name="opool", bufs=5))
        psum = ctx.enter_context(tc.psum_pool(name="psum", bufs=8))

        ident = const.tile([P, P], F32, name="ident")
        make_identity(nc, ident[:])
        heat = const.tile([P, 512], BF16, name="heat")
        nc.vector.memset(heat[:], 0.0)
        warm = const.tile([P, 2], F32, name="warm")
        nc.vector.memset(warm[:, 0:1], 0.0)
        nc.scalar.activation(out=warm[:, 1:2], in_=warm[:, 0:1], func=ACT.Copy)

        sc = const.tile([P, 2, 4], F32, name="sc")
        nc.sync.dma_start(out=sc[:], in_=W_attn_scale.rearrange("(g p t) o -> p g (t o)", p=P, t=4))
        wv = W_attn_bytes.rearrange("(g p t) n -> g p t n", p=P, t=4)
        xv = x.rearrange("o (p j) k -> p (o j) k", j=NJ)
        wby = {}
        xin = {}

        def load_w(b):
            for g in range(2):
                wt = const.tile([P, 4, 512], U8, name="wby%d_%d" % (b, g))
                wby[(b, g)] = wt
                if b == 0:
                    nc.sync.dma_start(out=wt[:], in_=wv[g][:, :, 0:512])
                elif b == 1:
                    nc.sync.dma_start(out=wt[:], in_=wv[g][:, :, 768:1280])
                else:
                    nc.sync.dma_start(out=wt[:, :, 0:256], in_=wv[g][:, :, 512:768])
                    nc.sync.dma_start(out=wt[:, :, 256:512], in_=wv[g][:, :, 1280:1536])

        def load_x(j):
            xt_in = const.tile([P, 1024], BF16, name="xin%d" % j)
            xin[j] = xt_in
            nc.sync.dma_start(out=xt_in[:], in_=xv[:, j, :])

        fq2 = const.tile([P, 2, 512, 2], BF16, name="fq2")
        fq = fq2[:, 0, :, :]
        fk = const.tile([P, 512, 2], BF16, name="fk")
        load_w(0)
        load_x(0)
        load_x(1)
        nc.sync.dma_start(out=fq.rearrange("p (s i) e -> p s (i e)", s=8),
                          in_=freqs_cis.rearrange("(s p) i e -> p s (i e)", p=P))
        load_w(1)
        for j in range(2, NJ):
            load_x(j)
        nc.sync.dma_start(out=fk[:].rearrange("p (g c) e -> p g (c e)", g=2),
                          in_=freqs_cis.rearrange("(g p a) i e -> p g (a i e)", p=P, a=4))
        load_w(2)

        wide = {}
        wgr = {}
        wc = {}
        wsc = {}

        def widen(eng, b, g, t):
            if t == 0:
                wide_t = wpool.tile([P, 4, 512], BF16, name="wide")
                wide[(b, g)] = wide_t
            src = wby[(b, g)][:, t, :].bitcast(FP8)
            dst = wide[(b, g)][:, t, :]
            s = sc[:, g, t:t + 1]
            if eng == "v":
                nc.vector.tensor_scalar(out=dst, in0=src, scalar1=s, scalar2=None, op0=ALU.mult)
            else:
                nc.scalar.activation(out=dst, in_=src, func=ACT.Copy, scale=s)

        def interleave(eng, b, g):
            wgr_t = wpool.tile([P, 512, 4], BF16, name="wgr", align_bytes=64)
            wgr[(b, g)] = wgr_t
            if b == 2:
                for v in range(2):
                    nc.scalar.copy(out=wgr_t[:, 256 * v:256 * (v + 1), :].rearrange("p (h f) t -> p h f t", h=2),
                                   in_=wide[(b, g)][:].rearrange("p t (h v f) -> p t h v f", h=2, v=2)[:, :, :, v, :]
                                   .rearrange("p t h f -> p h f t"))
                return
            src = wide[(b, g)][:].rearrange("p t (c i) -> p c t i", i=4)
            dst = wgr_t[:].rearrange("p (c i) t -> p c t i", i=4)
            if eng == "v":
                nc.vector.tensor_copy(out=dst, in_=src)
            else:
                nc.scalar.copy(out=dst, in_=src)

        def quant_w(b, g):
            c = const.tile([P, 512], U32, name="wc%d_%d" % (b, g), align_bytes=64)
            s = const.tile([P, 512], U8, name="ws%d_%d" % (b, g), align_bytes=64)
            wc[(b, g)] = c
            wsc[(b, g)] = s
            nc.vector.quantize_mx(out=c[:].bitcast(FP8X4), scales=s[:],
                                  in_=wgr[(b, g)][:].rearrange("p n t -> p (n t)"))

        xg = {}
        xc = {}
        xsc = {}

        def x_turn(j):
            xt = psum.tile([P, 2, 2, P], F32, name="acc")
            words = xin[j][:].bitcast(F32)
            for g in range(2):
                for u in range(2):
                    nc.tensor.transpose(xt[:, g, u, :], words[:, 256 * g + u:256 * (g + 1):2], ident[:])
            if j % 2 == 0:
                xg_t = xpool.tile([P, 2048], BF16, name="xg", align_bytes=64)
                xg[j // 2] = xg_t
            half = xg[j // 2][:, 1024 * (j % 2):1024 * (j % 2 + 1)]
            nc.scalar.copy(out=half.bitcast(F32).rearrange("p (g r u) -> p g r u", g=2, u=2),
                           in_=xt[:].rearrange("p g u r -> p g r u"))

        def x_quant(a, lo=0, hi=512):
            if a not in xc:
                c_t = const.tile([P, 512], U32, name="xc%d" % a, align_bytes=64)
                s_t = const.tile([P, 512], U8, name="xs%d" % a, align_bytes=64)
                xc[a] = c_t
                xsc[a] = s_t
            nc.vector.quantize_mx(out=xc[a][:, lo:hi].bitcast(FP8X4), scales=xsc[a][:, lo:hi], in_=xg[a][:, 4 * lo:4 * hi])

        def x_cols(j, g):
            return slice(256 * (j % 2) + P * g, 256 * (j % 2) + P * (g + 1))

        sk = const.tile([P, 512, 2], BF16, name="sk")
        qv = out_0.rearrange("o (s p) h f -> p (o s) (h f)", p=P)
        kv = out_1.rearrange("o (g p a) h f -> p (o g) (a h f)", p=P, a=4)
        vv = out_2.rearrange("o (g p a) h f -> p (o g) (a h f)", p=P, a=4)

        def mm(b, j):
            acc = psum.tile([P, 512], F32, name="acc")
            for g in range(2):
                nc.tensor.matmul_mx(out=acc[:],
                                    lhsT=xc[j // 2][:, x_cols(j, g)].bitcast(FP8X4),
                                    lhsT_scale=xsc[j // 2][:, x_cols(j, g)],
                                    rhs=wc[(b, g)][:].bitcast(FP8X4),
                                    rhs_scale=wsc[(b, g)][:],
                                    start=(g == 0), stop=(g == 1))
            return acc

        stage = {}

        def rope_q(b, j, acc):
            jj = j % JJ
            if jj == 0:
                oq_t = opool.tile([P, 4, JJ * P], F32, name="oq")
                stage["q"] = oq_t
            oq = stage["q"]
            t1 = tpool.tile([P, 256, 2], F32, name="t1")
            t2 = tpool.tile([P, 256, 2], F32, name="t2")
            av = acc[:].rearrange("p (c e) -> p c e", e=2)
            nc.vector.tensor_tensor(out=t1[:], in0=fq[:, 256 * b:256 * (b + 1), 0:1].to_broadcast([P, 256, 2]),
                                    in1=av, op=ALU.mult)
            nc.vector.tensor_tensor(out=t2[:], in0=fq2[:, ::-1, 256 * b:256 * (b + 1), 1].rearrange("p h c -> p c h"),
                                    in1=av[:, :, ::-1], op=ALU.mult)
            nc.gpsimd.tensor_tensor(out=oq[:, :, jj * P:(jj + 1) * P],
                                    in0=t1[:].rearrange("p (s i) e -> p s (i e)", s=4),
                                    in1=t2[:].rearrange("p (s i) e -> p s (i e)", s=4), op=ALU.add)
            if jj == JJ - 1:
                j0 = j - jj
                nc.sync.dma_start(out=qv[:, 4 * b:4 * (b + 1), j0 * P:(j + 1) * P], in_=oq[:])

        ck = const.tile([P, 512, 2], BF16, name="ck")

        def kv_pair(a):
            acc_k = psum.tile([P, 2, 256], F32, name="acc")
            acc_v = psum.tile([P, 2, 256], F32, name="acc")
            for jj in range(2):
                j = 2 * a + jj
                for v, acc in ((0, acc_k), (1, acc_v)):
                    for g in range(2):
                        nc.tensor.matmul_mx(out=acc[:, jj, :],
                                            lhsT=xc[a][:, x_cols(j, g)].bitcast(FP8X4),
                                            lhsT_scale=xsc[a][:, x_cols(j, g)],
                                            rhs=wc[(2, g)][:, 256 * v:256 * (v + 1)].bitcast(FP8X4),
                                            rhs_scale=wsc[(2, g)][:, 256 * v:256 * (v + 1)],
                                            start=(g == 0), stop=(g == 1))
            ok = opool.tile([P, 2, 2, P], F32, name="ok")
            ov = opool.tile([P, 2, 2, P], F32, name="ov")
            t1 = tpool.tile([P, 512], F32, name="t1")
            t2 = tpool.tile([P, 512], F32, name="t2")
            ckv = ck[:].rearrange("p (h a i) e -> p h a (i e)", h=2, a=4)[:, :, a, :].unsqueeze(1).to_broadcast([P, 2, 2, P])
            skv = sk[:].rearrange("p (h a i) e -> p h a (i e)", h=2, a=4)[:, :, a, :].unsqueeze(1).to_broadcast([P, 2, 2, P])
            nc.vector.tensor_tensor(out=t1[:].rearrange("p (j h f) -> p j h f", j=2, h=2),
                                    in0=ckv, in1=acc_k[:].rearrange("p j (h f) -> p j h f", h=2), op=ALU.mult)
            nc.vector.tensor_tensor(out=t2[:].rearrange("p (j h f) -> p j h f", j=2, h=2),
                                    in0=skv, in1=acc_k[:].rearrange("p j (c e) -> p (j c) e", e=2)[:, :, ::-1], op=ALU.mult)
            nc.scalar.copy(out=ov[:], in_=acc_v[:].rearrange("p j (h f) -> p h j f", h=2))
            okv = ok[:].rearrange("p h j f -> p j h f")
            t1v = t1[:].rearrange("p (j h f) -> p j h f", j=2, h=2)
            t2v = t2[:].rearrange("p (j h f) -> p j h f", j=2, h=2)
            cols = slice(2 * a * P, 2 * (a + 1) * P)
            nc.sync.dma_start(out=vv[:, :, cols], in_=ov[:].rearrange("p h j f -> p h (j f)"))

            def finish():
                nc.vector.tensor_tensor(out=okv, in0=t1v, in1=t2v, op=ALU.add)
                nc.sync.dma_start(out=kv[:, :, cols], in_=ok[:].rearrange("p h j f -> p h (j f)"))
            return finish

        hot = psum.tile([P, 512], F32, name="acc")
        for n in range(6):
            nc.tensor.matmul(out=hot[:], lhsT=heat[:, 0:P], rhs=heat[:], start=True, stop=True)
        for t in range(4):
            widen("v", 0, 0, t)
        widen("v", 0, 1, 0)
        for t in range(1, 4):
            widen("s", 0, 1, t)
        x_turn(0)
        x_turn(1)

        def keep_hot(g):
            for n in range(3):
                nc.tensor.matmul(out=hot[:], lhsT=heat[:, 0:P], rhs=wgr[(0, g)][:, 0:P, :].rearrange("p n t -> p (n t)"),
                                 start=True, stop=True)

        interleave("v", 0, 0)
        keep_hot(0)
        x_quant(0, 0, 256)
        quant_w(0, 0)
        interleave("v", 0, 1)
        keep_hot(1)
        x_quant(0, 256, 512)
        quant_w(0, 1)
        nc.scalar.activation(out=fq2[:, 1, :, 1:2], in_=fq2[:, 0, :, 1:2], func=ACT.Copy, scale=-1.0)

        def prep_items(b):
            items = []
            for g in range(2):
                for t in range(4):
                    items.append(("w", b, g, t))
                items.append(("i", b, g, 0))
                items.append(("q", b, g, 0))
            return items

        def run_item(it):
            kind, b, g, t = it
            if kind == "w":
                widen("s", b, g, t)
            elif kind == "i":
                interleave("v" if (b == 1 and g == 0) else "s", b, g)
            else:
                quant_w(b, g)

        for b in range(2):
            items = prep_items(b + 1)
            if b == 1:
                nc.scalar.activation(out=sk[:, :, 0:1], in_=fk[:, :, 1:2], func=ACT.Copy, scale=-1.0)
                nc.scalar.copy(out=sk[:, :, 1:2], in_=fk[:, :, 1:2])
                nc.scalar.copy(out=ck[:], in_=fk[:, :, 0:1].to_broadcast([P, 512, 2]))
            for j in range(NJ):
                if b == 0 and j % 2 == 0 and j + 2 < NJ:
                    x_turn(j + 2)
                    x_turn(j + 3)
                    x_quant(j // 2 + 1)
                acc = mm(b, j)
                rope_q(b, j, acc)
                for n in range(2):
                    if items:
                        run_item(items.pop(0))
        pending = []
        for a in range(4):
            pending.append(kv_pair(a))
            if a > 0:
                pending.pop(0)()
        pending.pop(0)()
